import numpy as np
import ml_dtypes


def mxq(x, axis, fmt="e4m3"):
    dtype, down = {"e4m3": (ml_dtypes.float8_e4m3fn, 7), "e5m2": (ml_dtypes.float8_e5m2, 14)}[fmt]
    v = np.moveaxis(np.asarray(x, np.float32).astype(ml_dtypes.bfloat16).astype(np.float64), axis, -1)
    blocks = v.reshape(v.shape[:-1] + (-1, 32))
    amax = np.abs(blocks).max(-1, keepdims=True)
    byte = np.maximum(np.where(amax > 0, np.frexp(amax)[1] - 1 + 127, 0) - down, 1)
    scale = np.exp2(byte - 127.0)
    codes = (blocks / scale).astype(np.float32).astype(dtype).astype(np.float64)
    return np.moveaxis((codes * scale).reshape(v.shape), -1, axis)


WIDE = False


def mx_kscale(k):
    if not WIDE:
        return np.ones(k)
    levels = np.array([20, -20, 10, -10, 0])
    a = np.random.permutation(np.resize(levels, k // 512 * 4)).reshape(k // 512, 4)
    idx = np.arange(k)
    return np.exp2(a[idx // 512, idx % 128 // 32])


BF16 = ml_dtypes.bfloat16


def bf(x):
    return np.asarray(x, np.float32).astype(BF16)


def f64(x):
    return np.asarray(x).astype(np.float64)


B, S, IN_F, OUT_F, GS = 4, 2048, 512, 512, 128
GPR = IN_F // GS
N_GROUPS = OUT_F * GPR


def build_weight(signs, scale_pos, scale_neg, gs):
    signs = f64(signs)
    out_f, in_f = signs.shape
    sp = np.repeat(f64(scale_pos), gs).reshape(out_f, in_f)
    sn = np.repeat(f64(scale_neg), gs).reshape(out_f, in_f)
    eff_scale = np.where(signs > 0, sp, sn)
    return signs * eff_scale


def setup_inputs():
    u = mx_kscale(OUT_F)
    uflat = np.repeat(u, GPR)
    lo, hi = 0.64 / np.sqrt(IN_F), 3.2 / np.sqrt(IN_F)
    x = np.random.standard_normal((B, S, IN_F))
    raw = np.random.standard_normal((OUT_F, IN_F))
    signs = np.where(raw >= 0, 1.0, -1.0)
    scale_pos = np.random.uniform(lo, hi, N_GROUPS) / uflat
    scale_neg = np.random.uniform(lo, hi, N_GROUPS) / uflat
    g = np.random.standard_normal((B, S, OUT_F)) * np.exp2(np.random.randint(-12, 1, (B, S, 1))) * u
    return {"x": bf(x), "signs": bf(signs), "scale_pos": bf(scale_pos), "scale_neg": bf(scale_neg), "gs": GS, "grad_out": bf(g)}


def reference(x, signs, scale_pos, scale_neg, gs, grad_out):
    weight = build_weight(signs, scale_pos, scale_neg, gs)
    return mxq(f64(grad_out), 2, "e5m2") @ mxq(weight, 0, "e4m3")

@@ -1,0 +1,146 @@
+from contextlib import ExitStack
+
+import concourse.masks as masks
+import concourse.mybir as mybir
+
+F32 = mybir.dt.float32
+BF16 = mybir.dt.bfloat16
+U32 = mybir.dt.uint32
+U8 = mybir.dt.uint8
+E4M3X4 = mybir.dt.float8_e4m3fn_x4
+E5M2X4 = mybir.dt.float8_e5m2_x4
+ALU = mybir.AluOpType
+
+P = 128
+TOKENS = 4 * 2048
+OUT_F = 512
+IN_F = 512
+FLOPS = 2 * TOKENS * OUT_F * IN_F
+BYTES = TOKENS * OUT_F * 2 + OUT_F * IN_F * 2 + 2 * 2048 * 2 + TOKENS * IN_F * 4
+
+J = TOKENS // P
+GROUP = 4
+N_GROUPS = J // GROUP
+LOADS = [4, 4, 8, 16, 16, 16]
+STORE = 8
+MANUAL = False
+VEC_OUT = {(1, 3)}
+
+
+def tile_signcondpackedbitlinear_t_kernel(tc, x, signs, scale_pos, scale_neg, gs, grad_out, out):
+    nc = tc.nc
+    gpr = IN_F // gs
+    n_sc = 4 * gpr
+    g_flat = grad_out.flatten_outer_dims().rearrange("(p j) k -> p (j k)", j=J)
+    o_flat = out.flatten_outer_dims().rearrange("(p j) i -> p (j i)", j=J)
+
+    with ExitStack() as ctx:
+        keep = ctx.enter_context(tc.tile_pool(name="keep", bufs=1))
+        stage = ctx.enter_context(tc.tile_pool(name="stage", bufs=3))
+        opool = ctx.enter_context(tc.tile_pool(name="opool", bufs=6))
+        tpsum = ctx.enter_context(tc.psum_pool(name="tpsum", bufs=4))
+        apsum = ctx.enter_context(tc.psum_pool(name="apsum", bufs=4))
+        if MANUAL:
+            ctx.enter_context(tc.manual_schedule())
+
+        sp_sb = keep.tile([P, n_sc], BF16, name="sp_sb")
+        sn_sb = keep.tile([P, n_sc], BF16, name="sn_sb")
+        nc.scalar.dma_start(out=sp_sb[:].rearrange("q (u r) -> q u r", u=2),
+                            in_=scale_pos.rearrange("(u q r) -> q u r", u=2, q=P))
+        nc.scalar.dma_start(out=sn_sb[:].rearrange("q (u r) -> q u r", u=2),
+                            in_=scale_neg.rearrange("(u q r) -> q u r", u=2, q=P))
+        s_sb = keep.tile([P, 4 * IN_F], BF16, name="s_sb")
+        nc.sync.dma_start(out=s_sb[:].rearrange("q (u r) -> q u r", u=2),
+                          in_=signs.rearrange("(u q e) i -> q u (e i)", u=2, q=P, e=2))
+        g32 = []
+        j0 = 0
+        for c, nj in enumerate(LOADS):
+            g_sb = keep.tile([P, nj * OUT_F], BF16, name="g_sb%d" % c)
+            nc.sync.dma_start(out=g_sb[:], in_=g_flat[:, j0 * OUT_F:(j0 + nj) * OUT_F])
+            for jj in range(nj):
+                g32.append((g_sb[:].bitcast(F32), jj * (OUT_F // 2)))
+            j0 += nj
+
+        ident = keep.tile([P, P], F32, name="ident")
+        masks.make_identity(nc, ident[:])
+
+        w_codes = keep.tile([P, IN_F], U32, name="w_codes", align_bytes=64)
+        w_scales = keep.tile([P, IN_F], U8, name="w_scales", align_bytes=64)
+
+        def build_weight():
+            a_sb = keep.tile([P, 4 * IN_F], BF16, name="a_sb")
+            b_sb = keep.tile([P, 4 * IN_F], BF16, name="b_sb")
+            wg = keep.tile([P, IN_F, 4], BF16, name="wg", align_bytes=64)
+            s_v = s_sb[:].rearrange("q (g c) -> q g c", c=gs)
+            nc.vector.scalar_tensor_tensor(
+                out=a_sb[:].rearrange("q (g c) -> q g c", c=gs), in0=s_v, scalar=0.0,
+                in1=sp_sb[:].unsqueeze(2).to_broadcast([P, n_sc, gs]), op0=ALU.max, op1=ALU.mult)
+            nc.vector.scalar_tensor_tensor(
+                out=b_sb[:].rearrange("q (g c) -> q g c", c=gs), in0=s_v, scalar=0.0,
+                in1=sn_sb[:].unsqueeze(2).to_broadcast([P, n_sc, gs]), op0=ALU.min, op1=ALU.mult)
+            nc.vector.tensor_tensor(
+                out=wg[:], in0=a_sb[:].rearrange("q (t i) -> q i t", t=4),
+                in1=b_sb[:].rearrange("q (t i) -> q i t", t=4), op=ALU.add)
+            nc.vector.quantize_mx(out=w_codes[:].bitcast(E4M3X4), scales=w_scales[:],
+                                  in_=wg[:].rearrange("q i t -> q (i t)"))
+
+        grouped = {}
+        codes = {}
+        planes = {}
+
+        def transposes(n):
+            grp = stage.tile([P, GROUP * P * 4], BF16, name="grp", align_bytes=64)
+            grouped[n] = grp
+            grp32 = grp[:].bitcast(F32)
+            for h in range(GROUP // 2):
+                xt = tpsum.tile([P, 2, 2 * P], F32, name="xt")
+                for jj in range(2):
+                    view, off = g32[n * GROUP + 2 * h + jj]
+                    for u in range(2):
+                        nc.tensor.transpose(xt[:, u, jj * P:(jj + 1) * P],
+                                            view[:, off + u * P: off + (u + 1) * P], ident[:])
+                nc.vector.tensor_copy(
+                    out=grp32[:, h * 4 * P:(h + 1) * 4 * P].rearrange("q (c u) -> q c u", u=2),
+                    in_=xt[:].rearrange("q u c -> q c u"))
+
+        def quantise(n):
+            cd = stage.tile([P, GROUP * P], U32, name="cd", align_bytes=64)
+            pl = stage.tile([P, GROUP * P], U8, name="pl", align_bytes=64)
+            codes[n] = cd
+            planes[n] = pl
+            nc.vector.quantize_mx(out=cd[:].bitcast(E5M2X4), scales=pl[:], in_=grouped[n][:])
+
+        o_tiles = {}
+
+        def multiply(n):
+            per = STORE // GROUP
+            if n % per == 0:
+                o_new = opool.tile([P, STORE * IN_F], F32, name="o_sb")
+                o_tiles[n // per] = o_new
+            o_sb = o_tiles[n // per]
+            for i in range(GROUP):
+                acc = apsum.tile([P, IN_F], F32, name="acc")
+                nc.tensor.matmul_mx(
+                    out=acc[:],
+                    lhsT=codes[n][:, i * P:(i + 1) * P].bitcast(E5M2X4),
+                    lhsT_scale=planes[n][:, i * P:(i + 1) * P],
+                    rhs=w_codes[:].bitcast(E4M3X4), rhs_scale=w_scales[:],
+                    start=True, stop=True)
+                col = ((n % per) * GROUP + i) * IN_F
+                if (n % 2, i) in VEC_OUT:
+                    nc.vector.tensor_copy(out=o_sb[:, col:col + IN_F], in_=acc[:])
+                else:
+                    nc.scalar.copy(out=o_sb[:, col:col + IN_F], in_=acc[:])
+            if n % per == per - 1:
+                c0 = (n // per) * STORE * IN_F
+                nc.sync.dma_start(out=o_flat[:, c0:c0 + STORE * IN_F], in_=o_sb[:])
+
+        build_weight()
+        transposes(0)
+        quantise(0)
+        for n in range(N_GROUPS):
+            if n + 1 < N_GROUPS:
+                transposes(n + 1)
+            multiply(n)
+            if n + 1 < N_GROUPS:
+                quantise(n + 1)

@@ -22,9 +22,10 @@ J = TOKENS // P
 GROUP = 4
 N_GROUPS = J // GROUP
 LOADS = [4, 4, 8, 16, 16, 16]
-STORE = 8
-MANUAL = False
+MANUAL = True
 VEC_OUT = {(1, 3)}
+N_EARLY = 3
+STORES = [8, 8, 8, 8, 8, 8, 8, 4, 4]
 
 
 def tile_signcondpackedbitlinear_t_kernel(tc, x, signs, scale_pos, scale_neg, gs, grad_out, out):
@@ -36,7 +37,8 @@ def tile_signcondpackedbitlinear_t_kernel(tc, x, signs, scale_pos, scale_neg, gs
 
     with ExitStack() as ctx:
         keep = ctx.enter_context(tc.tile_pool(name="keep", bufs=1))
-        stage = ctx.enter_context(tc.tile_pool(name="stage", bufs=3))
+        stage = ctx.enter_context(tc.tile_pool(name="stage", bufs=4))
+        gpool = ctx.enter_context(tc.tile_pool(name="gpool", bufs=6))
         opool = ctx.enter_context(tc.tile_pool(name="opool", bufs=6))
         tpsum = ctx.enter_context(tc.psum_pool(name="tpsum", bufs=4))
         apsum = ctx.enter_context(tc.psum_pool(name="apsum", bufs=4))
@@ -89,7 +91,7 @@ def tile_signcondpackedbitlinear_t_kernel(tc, x, signs, scale_pos, scale_neg, gs
         planes = {}
 
         def transposes(n):
-            grp = stage.tile([P, GROUP * P * 4], BF16, name="grp", align_bytes=64)
+            grp = gpool.tile([P, GROUP * P * 4], BF16, name="grp", align_bytes=64)
             grouped[n] = grp
             grp32 = grp[:].bitcast(F32)
             for h in range(GROUP // 2):
@@ -99,9 +101,9 @@ def tile_signcondpackedbitlinear_t_kernel(tc, x, signs, scale_pos, scale_neg, gs
                     for u in range(2):
                         nc.tensor.transpose(xt[:, u, jj * P:(jj + 1) * P],
                                             view[:, off + u * P: off + (u + 1) * P], ident[:])
-                nc.vector.tensor_copy(
-                    out=grp32[:, h * 4 * P:(h + 1) * 4 * P].rearrange("q (c u) -> q c u", u=2),
-                    in_=xt[:].rearrange("q u c -> q c u"))
+                copier = nc.scalar.copy if n < N_EARLY else nc.vector.tensor_copy
+                copier(out=grp32[:, h * 4 * P:(h + 1) * 4 * P].rearrange("q (c u) -> q c u", u=2),
+                       in_=xt[:].rearrange("q u c -> q c u"))
 
         def quantise(n):
             cd = stage.tile([P, GROUP * P], U32, name="cd", align_bytes=64)
@@ -110,15 +112,20 @@ def tile_signcondpackedbitlinear_t_kernel(tc, x, signs, scale_pos, scale_neg, gs
             planes[n] = pl
             nc.vector.quantize_mx(out=cd[:].bitcast(E5M2X4), scales=pl[:], in_=grouped[n][:])
 
+        store_of = []
+        for k, width in enumerate(STORES):
+            for pos in range(width):
+                store_of.append((k, pos))
         o_tiles = {}
 
         def multiply(n):
-            per = STORE // GROUP
-            if n % per == 0:
-                o_new = opool.tile([P, STORE * IN_F], F32, name="o_sb")
-                o_tiles[n // per] = o_new
-            o_sb = o_tiles[n // per]
             for i in range(GROUP):
+                j = n * GROUP + i
+                k, pos = store_of[j]
+                if pos == 0:
+                    o_new = opool.tile([P, STORES[k] * IN_F], F32, name="o_sb", tag="o_sb")
+                    o_tiles[k] = o_new
+                o_sb = o_tiles[k]
                 acc = apsum.tile([P, IN_F], F32, name="acc")
                 nc.tensor.matmul_mx(
                     out=acc[:],
@@ -126,21 +133,22 @@ def tile_signcondpackedbitlinear_t_kernel(tc, x, signs, scale_pos, scale_neg, gs
                     lhsT_scale=planes[n][:, i * P:(i + 1) * P],
                     rhs=w_codes[:].bitcast(E4M3X4), rhs_scale=w_scales[:],
                     start=True, stop=True)
-                col = ((n % per) * GROUP + i) * IN_F
                 if (n % 2, i) in VEC_OUT:
-                    nc.vector.tensor_copy(out=o_sb[:, col:col + IN_F], in_=acc[:])
+                    nc.vector.tensor_copy(out=o_sb[:, pos * IN_F:(pos + 1) * IN_F], in_=acc[:])
                 else:
-                    nc.scalar.copy(out=o_sb[:, col:col + IN_F], in_=acc[:])
-            if n % per == per - 1:
-                c0 = (n // per) * STORE * IN_F
-                nc.sync.dma_start(out=o_flat[:, c0:c0 + STORE * IN_F], in_=o_sb[:])
+                    nc.scalar.copy(out=o_sb[:, pos * IN_F:(pos + 1) * IN_F], in_=acc[:])
+                if pos == STORES[k] - 1:
+                    c0 = (j + 1 - STORES[k]) * IN_F
+                    nc.sync.dma_start(out=o_flat[:, c0:c0 + STORES[k] * IN_F], in_=o_sb[:])
 
         build_weight()
-        transposes(0)
+        for n in range(N_EARLY):
+            transposes(n)
         quantise(0)
+        quantise(1)
         for n in range(N_GROUPS):
-            if n + 1 < N_GROUPS:
-                transposes(n + 1)
+            if n + 2 < N_GROUPS:
+                quantise(n + 2)
+            if n + N_EARLY < N_GROUPS:
+                transposes(n + N_EARLY)
             multiply(n)
-            if n + 1 < N_GROUPS:
-                quantise(n + 1)

@@ -22,10 +22,10 @@ J = TOKENS // P
 GROUP = 4
 N_GROUPS = J // GROUP
 LOADS = [4, 4, 8, 16, 16, 16]
+N_TAIL = 3
 MANUAL = True
-VEC_OUT = {(1, 3)}
 N_EARLY = 3
-STORES = [8, 8, 8, 8, 8, 8, 8, 4, 4]
+STORES = [4, 4, 8, 8, 8, 8, 8, 8, 4, 4]
 
 
 def tile_signcondpackedbitlinear_t_kernel(tc, x, signs, scale_pos, scale_neg, gs, grad_out, out):
@@ -51,9 +51,12 @@ def tile_signcondpackedbitlinear_t_kernel(tc, x, signs, scale_pos, scale_neg, gs
                             in_=scale_pos.rearrange("(u q r) -> q u r", u=2, q=P))
         nc.scalar.dma_start(out=sn_sb[:].rearrange("q (u r) -> q u r", u=2),
                             in_=scale_neg.rearrange("(u q r) -> q u r", u=2, q=P))
-        s_sb = keep.tile([P, 4 * IN_F], BF16, name="s_sb")
-        nc.sync.dma_start(out=s_sb[:].rearrange("q (u r) -> q u r", u=2),
-                          in_=signs.rearrange("(u q e) i -> q u (e i)", u=2, q=P, e=2))
+        s_view = signs.rearrange("(u q e) i -> u q (e i)", u=2, q=P, e=2)
+        s_half = []
+        for u in range(2):
+            s_sb = keep.tile([P, 2 * IN_F], BF16, name="s_sb%d" % u)
+            nc.sync.dma_start(out=s_sb[:], in_=s_view[u, :, :])
+            s_half.append(s_sb)
         g32 = []
         j0 = 0
         for c, nj in enumerate(LOADS):
@@ -69,20 +72,26 @@ def tile_signcondpackedbitlinear_t_kernel(tc, x, signs, scale_pos, scale_neg, gs
         w_codes = keep.tile([P, IN_F], U32, name="w_codes", align_bytes=64)
         w_scales = keep.tile([P, IN_F], U8, name="w_scales", align_bytes=64)
 
+        wg = keep.tile([P, IN_F, 4], BF16, name="wg", align_bytes=64)
+
         def build_weight():
+            spf = keep.tile([P, n_sc], F32, name="spf")
+            snf = keep.tile([P, n_sc], F32, name="snf")
+            nc.vector.tensor_copy(out=spf[:], in_=sp_sb[:])
+            nc.vector.tensor_copy(out=snf[:], in_=sn_sb[:])
             a_sb = keep.tile([P, 4 * IN_F], BF16, name="a_sb")
             b_sb = keep.tile([P, 4 * IN_F], BF16, name="b_sb")
-            wg = keep.tile([P, IN_F, 4], BF16, name="wg", align_bytes=64)
-            s_v = s_sb[:].rearrange("q (g c) -> q g c", c=gs)
-            nc.vector.scalar_tensor_tensor(
-                out=a_sb[:].rearrange("q (g c) -> q g c", c=gs), in0=s_v, scalar=0.0,
-                in1=sp_sb[:].unsqueeze(2).to_broadcast([P, n_sc, gs]), op0=ALU.max, op1=ALU.mult)
-            nc.vector.scalar_tensor_tensor(
-                out=b_sb[:].rearrange("q (g c) -> q g c", c=gs), in0=s_v, scalar=0.0,
-                in1=sn_sb[:].unsqueeze(2).to_broadcast([P, n_sc, gs]), op0=ALU.min, op1=ALU.mult)
-            nc.vector.tensor_tensor(
-                out=wg[:], in0=a_sb[:].rearrange("q (t i) -> q i t", t=4),
-                in1=b_sb[:].rearrange("q (t i) -> q i t", t=4), op=ALU.add)
+            for g in range(n_sc):
+                src = s_half[g // (n_sc // 2)][:, (g % (n_sc // 2)) * gs:(g % (n_sc // 2) + 1) * gs]
+                nc.vector.tensor_scalar(out=a_sb[:, g * gs:(g + 1) * gs], in0=src, scalar1=0.0,
+                                        scalar2=spf[:, g:g + 1], op0=ALU.max, op1=ALU.mult)
+                nc.vector.tensor_scalar(out=b_sb[:, g * gs:(g + 1) * gs], in0=src, scalar1=0.0,
+                                        scalar2=snf[:, g:g + 1], op0=ALU.min, op1=ALU.mult)
+            nc.vector.tensor_tensor(out=a_sb[:], in0=a_sb[:], in1=b_sb[:], op=ALU.add)
+            nc.vector.tensor_copy(out=wg[:].rearrange("q (c i) t -> q c t i", i=4),
+                                  in_=a_sb[:].rearrange("q (t c i) -> q c t i", t=4, i=4))
+
+        def quantise_weight():
             nc.vector.quantize_mx(out=w_codes[:].bitcast(E4M3X4), scales=w_scales[:],
                                   in_=wg[:].rearrange("q i t -> q (i t)"))
 
@@ -133,7 +142,7 @@ def tile_signcondpackedbitlinear_t_kernel(tc, x, signs, scale_pos, scale_neg, gs
                     lhsT_scale=planes[n][:, i * P:(i + 1) * P],
                     rhs=w_codes[:].bitcast(E4M3X4), rhs_scale=w_scales[:],
                     start=True, stop=True)
-                if (n % 2, i) in VEC_OUT:
+                if (i % 2 == 1) if n >= N_GROUPS - N_TAIL else (i == 3 and n % 4 == 1):
                     nc.vector.tensor_copy(out=o_sb[:, pos * IN_F:(pos + 1) * IN_F], in_=acc[:])
                 else:
                     nc.scalar.copy(out=o_sb[:, pos * IN_F:(pos + 1) * IN_F], in_=acc[:])
@@ -145,6 +154,7 @@ def tile_signcondpackedbitlinear_t_kernel(tc, x, signs, scale_pos, scale_neg, gs
         for n in range(N_EARLY):
             transposes(n)
         quantise(0)
+        quantise_weight()
         quantise(1)
         for n in range(N_GROUPS):
             if n + 2 < N_GROUPS:

@@ -25,7 +25,7 @@ LOADS = [4, 4, 8, 16, 16, 16]
 N_TAIL = 3
 MANUAL = True
 N_EARLY = 3
-STORES = [4, 4, 8, 8, 8, 8, 8, 8, 4, 4]
+STORES = [4, 4, 8, 8, 8, 8, 8, 8, 4, 2, 1, 1]
 
 
 def tile_signcondpackedbitlinear_t_kernel(tc, x, signs, scale_pos, scale_neg, gs, grad_out, out):

@@ -47,16 +47,10 @@ def tile_signcondpackedbitlinear_t_kernel(tc, x, signs, scale_pos, scale_neg, gs
 
         sp_sb = keep.tile([P, n_sc], BF16, name="sp_sb")
         sn_sb = keep.tile([P, n_sc], BF16, name="sn_sb")
-        nc.scalar.dma_start(out=sp_sb[:].rearrange("q (u r) -> q u r", u=2),
-                            in_=scale_pos.rearrange("(u q r) -> q u r", u=2, q=P))
-        nc.scalar.dma_start(out=sn_sb[:].rearrange("q (u r) -> q u r", u=2),
-                            in_=scale_neg.rearrange("(u q r) -> q u r", u=2, q=P))
-        s_view = signs.rearrange("(u q e) i -> u q (e i)", u=2, q=P, e=2)
-        s_half = []
-        for u in range(2):
-            s_sb = keep.tile([P, 2 * IN_F], BF16, name="s_sb%d" % u)
-            nc.sync.dma_start(out=s_sb[:], in_=s_view[u, :, :])
-            s_half.append(s_sb)
+        nc.scalar.dma_start(out=sp_sb[:], in_=scale_pos.rearrange("(q r) -> q r", q=P))
+        nc.scalar.dma_start(out=sn_sb[:], in_=scale_neg.rearrange("(q r) -> q r", q=P))
+        s_sb = keep.tile([P, 4 * IN_F], BF16, name="s_sb")
+        nc.sync.dma_start(out=s_sb[:], in_=signs.rearrange("(q t) i -> q (t i)", t=4))
         g32 = []
         j0 = 0
         for c, nj in enumerate(LOADS):
@@ -82,7 +76,7 @@ def tile_signcondpackedbitlinear_t_kernel(tc, x, signs, scale_pos, scale_neg, gs
             a_sb = keep.tile([P, 4 * IN_F], BF16, name="a_sb")
             b_sb = keep.tile([P, 4 * IN_F], BF16, name="b_sb")
             for g in range(n_sc):
-                src = s_half[g // (n_sc // 2)][:, (g % (n_sc // 2)) * gs:(g % (n_sc // 2) + 1) * gs]
+                src = s_sb[:, g * gs:(g + 1) * gs]
                 nc.vector.tensor_scalar(out=a_sb[:, g * gs:(g + 1) * gs], in0=src, scalar1=0.0,
                                         scalar2=spf[:, g:g + 1], op0=ALU.max, op1=ALU.mult)
                 nc.vector.tensor_scalar(out=b_sb[:, g * gs:(g + 1) * gs], in0=src, scalar1=0.0,
@@ -109,7 +103,7 @@ def tile_signcondpackedbitlinear_t_kernel(tc, x, signs, scale_pos, scale_neg, gs
                     view, off = g32[n * GROUP + 2 * h + jj]
                     for u in range(2):
                         nc.tensor.transpose(xt[:, u, jj * P:(jj + 1) * P],
-                                            view[:, off + u * P: off + (u + 1) * P], ident[:])
+                                            view[:, off + u: off + 2 * P: 2], ident[:])
                 copier = nc.scalar.copy if n < N_EARLY else nc.vector.tensor_copy
                 copier(out=grp32[:, h * 4 * P:(h + 1) * 4 * P].rearrange("q (c u) -> q c u", u=2),
                        in_=xt[:].rearrange("q u c -> q c u"))

@@ -49,12 +49,12 @@ def tile_signcondpackedbitlinear_t_kernel(tc, x, signs, scale_pos, scale_neg, gs
         sn_sb = keep.tile([P, n_sc], BF16, name="sn_sb")
         nc.scalar.dma_start(out=sp_sb[:], in_=scale_pos.rearrange("(q r) -> q r", q=P))
         nc.scalar.dma_start(out=sn_sb[:], in_=scale_neg.rearrange("(q r) -> q r", q=P))
-        s_sb = keep.tile([P, 4 * IN_F], BF16, name="s_sb")
+        s_sb = keep.tile([P, 4 * IN_F], BF16, name="s_sb", align_bytes=256)
         nc.sync.dma_start(out=s_sb[:], in_=signs.rearrange("(q t) i -> q (t i)", t=4))
         g32 = []
         j0 = 0
         for c, nj in enumerate(LOADS):
-            g_sb = keep.tile([P, nj * OUT_F], BF16, name="g_sb%d" % c)
+            g_sb = keep.tile([P, nj * OUT_F], BF16, name="g_sb%d" % c, align_bytes=256)
             nc.sync.dma_start(out=g_sb[:], in_=g_flat[:, j0 * OUT_F:(j0 + nj) * OUT_F])
             for jj in range(nj):
                 g32.append((g_sb[:].bitcast(F32), jj * (OUT_F // 2)))
@@ -126,7 +126,7 @@ def tile_signcondpackedbitlinear_t_kernel(tc, x, signs, scale_pos, scale_neg, gs
                 j = n * GROUP + i
                 k, pos = store_of[j]
                 if pos == 0:
-                    o_new = opool.tile([P, STORES[k] * IN_F], F32, name="o_sb", tag="o_sb")
+                    o_new = opool.tile([P, STORES[k] * IN_F], F32, name="o_sb", tag="o_sb", align_bytes=256)
                     o_tiles[k] = o_new
                 o_sb = o_tiles[k]
                 acc = apsum.tile([P, IN_F], F32, name="acc")

@@ -21,11 +21,11 @@ BYTES = TOKENS * OUT_F * 2 + OUT_F * IN_F * 2 + 2 * 2048 * 2 + TOKENS * IN_F * 4
 J = TOKENS // P
 GROUP = 4
 N_GROUPS = J // GROUP
-LOADS = [4, 4, 8, 16, 16, 16]
+LOADS = [8, 8, 16, 32]
 N_TAIL = 3
 MANUAL = True
 N_EARLY = 3
-STORES = [4, 4, 8, 8, 8, 8, 8, 8, 4, 2, 1, 1]
+STORES = [8, 8, 8, 8, 8, 8, 8, 8]
 
 
 def tile_signcondpackedbitlinear_t_kernel(tc, x, signs, scale_pos, scale_neg, gs, grad_out, out):

@@ -49,12 +49,12 @@ def tile_signcondpackedbitlinear_t_kernel(tc, x, signs, scale_pos, scale_neg, gs
         sn_sb = keep.tile([P, n_sc], BF16, name="sn_sb")
         nc.scalar.dma_start(out=sp_sb[:], in_=scale_pos.rearrange("(q r) -> q r", q=P))
         nc.scalar.dma_start(out=sn_sb[:], in_=scale_neg.rearrange("(q r) -> q r", q=P))
-        s_sb = keep.tile([P, 4 * IN_F], BF16, name="s_sb", align_bytes=256)
+        s_sb = keep.tile([P, 4 * IN_F], BF16, name="s_sb", align_bytes=4096)
         nc.sync.dma_start(out=s_sb[:], in_=signs.rearrange("(q t) i -> q (t i)", t=4))
         g32 = []
         j0 = 0
         for c, nj in enumerate(LOADS):
-            g_sb = keep.tile([P, nj * OUT_F], BF16, name="g_sb%d" % c, align_bytes=256)
+            g_sb = keep.tile([P, nj * OUT_F], BF16, name="g_sb%d" % c, align_bytes=4096)
             nc.sync.dma_start(out=g_sb[:], in_=g_flat[:, j0 * OUT_F:(j0 + nj) * OUT_F])
             for jj in range(nj):
                 g32.append((g_sb[:].bitcast(F32), jj * (OUT_F // 2)))
@@ -126,7 +126,7 @@ def tile_signcondpackedbitlinear_t_kernel(tc, x, signs, scale_pos, scale_neg, gs
                 j = n * GROUP + i
                 k, pos = store_of[j]
                 if pos == 0:
-                    o_new = opool.tile([P, STORES[k] * IN_F], F32, name="o_sb", tag="o_sb", align_bytes=256)
+                    o_new = opool.tile([P, STORES[k] * IN_F], F32, name="o_sb", tag="o_sb", align_bytes=4096)
                     o_tiles[k] = o_new
                 o_sb = o_tiles[k]
                 acc = apsum.tile([P, IN_F], F32, name="acc")

from contextlib import ExitStack

import concourse.masks as masks
import concourse.mybir as mybir

F32 = mybir.dt.float32
BF16 = mybir.dt.bfloat16
U32 = mybir.dt.uint32
U8 = mybir.dt.uint8
E4M3X4 = mybir.dt.float8_e4m3fn_x4
E5M2X4 = mybir.dt.float8_e5m2_x4
ALU = mybir.AluOpType

P = 128
TOKENS = 4 * 2048
OUT_F = 512
IN_F = 512
FLOPS = 2 * TOKENS * OUT_F * IN_F
BYTES = TOKENS * OUT_F * 2 + OUT_F * IN_F * 2 + 2 * 2048 * 2 + TOKENS * IN_F * 4

J = TOKENS // P
GROUP = 4
N_GROUPS = J // GROUP
LOADS = [8, 8, 16, 32]
N_TAIL = 3
MANUAL = True
N_EARLY = 3
STORES = [8, 8, 8, 8, 8, 8, 8, 8]


def tile_signcondpackedbitlinear_t_kernel(tc, x, signs, scale_pos, scale_neg, gs, grad_out, out):
    nc = tc.nc
    gpr = IN_F // gs
    n_sc = 4 * gpr
    g_flat = grad_out.flatten_outer_dims().rearrange("(p j) k -> p (j k)", j=J)
    o_flat = out.flatten_outer_dims().rearrange("(p j) i -> p (j i)", j=J)

    with ExitStack() as ctx:
        keep = ctx.enter_context(tc.tile_pool(name="keep", bufs=1))
        stage = ctx.enter_context(tc.tile_pool(name="stage", bufs=4))
        gpool = ctx.enter_context(tc.tile_pool(name="gpool", bufs=6))
        opool = ctx.enter_context(tc.tile_pool(name="opool", bufs=6))
        tpsum = ctx.enter_context(tc.psum_pool(name="tpsum", bufs=4))
        apsum = ctx.enter_context(tc.psum_pool(name="apsum", bufs=4))
        if MANUAL:
            ctx.enter_context(tc.manual_schedule())

        sp_sb = keep.tile([P, n_sc], BF16, name="sp_sb")
        sn_sb = keep.tile([P, n_sc], BF16, name="sn_sb")
        nc.scalar.dma_start(out=sp_sb[:], in_=scale_pos.rearrange("(q r) -> q r", q=P))
        nc.scalar.dma_start(out=sn_sb[:], in_=scale_neg.rearrange("(q r) -> q r", q=P))
        s_sb = keep.tile([P, 4 * IN_F], BF16, name="s_sb", align_bytes=4096)
        nc.sync.dma_start(out=s_sb[:], in_=signs.rearrange("(q t) i -> q (t i)", t=4))
        g32 = []
        j0 = 0
        for c, nj in enumerate(LOADS):
            g_sb = keep.tile([P, nj * OUT_F], BF16, name="g_sb%d" % c, align_bytes=4096)
            nc.sync.dma_start(out=g_sb[:], in_=g_flat[:, j0 * OUT_F:(j0 + nj) * OUT_F])
            for jj in range(nj):
                g32.append((g_sb[:].bitcast(F32), jj * (OUT_F // 2)))
            j0 += nj

        ident = keep.tile([P, P], F32, name="ident")
        masks.make_identity(nc, ident[:])

        w_codes = keep.tile([P, IN_F], U32, name="w_codes", align_bytes=64)
        w_scales = keep.tile([P, IN_F], U8, name="w_scales", align_bytes=64)

        wg = keep.tile([P, IN_F, 4], BF16, name="wg", align_bytes=64)

        def build_weight():
            spf = keep.tile([P, n_sc], F32, name="spf")
            snf = keep.tile([P, n_sc], F32, name="snf")
            nc.vector.tensor_copy(out=spf[:], in_=sp_sb[:])
            nc.vector.tensor_copy(out=snf[:], in_=sn_sb[:])
            a_sb = keep.tile([P, 4 * IN_F], BF16, name="a_sb")
            b_sb = keep.tile([P, 4 * IN_F], BF16, name="b_sb")
            for g in range(n_sc):
                src = s_sb[:, g * gs:(g + 1) * gs]
                nc.vector.tensor_scalar(out=a_sb[:, g * gs:(g + 1) * gs], in0=src, scalar1=0.0,
                                        scalar2=spf[:, g:g + 1], op0=ALU.max, op1=ALU.mult)
                nc.vector.tensor_scalar(out=b_sb[:, g * gs:(g + 1) * gs], in0=src, scalar1=0.0,
                                        scalar2=snf[:, g:g + 1], op0=ALU.min, op1=ALU.mult)
            nc.vector.tensor_tensor(out=a_sb[:], in0=a_sb[:], in1=b_sb[:], op=ALU.add)
            nc.vector.tensor_copy(out=wg[:].rearrange("q (c i) t -> q c t i", i=4),
                                  in_=a_sb[:].rearrange("q (t c i) -> q c t i", t=4, i=4))

        def quantise_weight():
            nc.vector.quantize_mx(out=w_codes[:].bitcast(E4M3X4), scales=w_scales[:],
                                  in_=wg[:].rearrange("q i t -> q (i t)"))

        grouped = {}
        codes = {}
        planes = {}

        def transposes(n):
            grp = gpool.tile([P, GROUP * P * 4], BF16, name="grp", align_bytes=64)
            grouped[n] = grp
            grp32 = grp[:].bitcast(F32)
            for h in range(GROUP // 2):
                xt = tpsum.tile([P, 2, 2 * P], F32, name="xt")
                for jj in range(2):
                    view, off = g32[n * GROUP + 2 * h + jj]
                    for u in range(2):
                        nc.tensor.transpose(xt[:, u, jj * P:(jj + 1) * P],
                                            view[:, off + u: off + 2 * P: 2], ident[:])
                copier = nc.scalar.copy if n < N_EARLY else nc.vector.tensor_copy
                copier(out=grp32[:, h * 4 * P:(h + 1) * 4 * P].rearrange("q (c u) -> q c u", u=2),
                       in_=xt[:].rearrange("q u c -> q c u"))

        def quantise(n):
            cd = stage.tile([P, GROUP * P], U32, name="cd", align_bytes=64)
            pl = stage.tile([P, GROUP * P], U8, name="pl", align_bytes=64)
            codes[n] = cd
            planes[n] = pl
            nc.vector.quantize_mx(out=cd[:].bitcast(E5M2X4), scales=pl[:], in_=grouped[n][:])

        store_of = []
        for k, width in enumerate(STORES):
            for pos in range(width):
                store_of.append((k, pos))
        o_tiles = {}

        def multiply(n):
            for i in range(GROUP):
                j = n * GROUP + i
                k, pos = store_of[j]
                if pos == 0:
                    o_new = opool.tile([P, STORES[k] * IN_F], F32, name="o_sb", tag="o_sb", align_bytes=4096)
                    o_tiles[k] = o_new
                o_sb = o_tiles[k]
                acc = apsum.tile([P, IN_F], F32, name="acc")
                nc.tensor.matmul_mx(
                    out=acc[:],
                    lhsT=codes[n][:, i * P:(i + 1) * P].bitcast(E5M2X4),
                    lhsT_scale=planes[n][:, i * P:(i + 1) * P],
                    rhs=w_codes[:].bitcast(E4M3X4), rhs_scale=w_scales[:],
                    start=True, stop=True)
                if (i % 2 == 1) if n >= N_GROUPS - N_TAIL else (i == 3 and n % 4 == 1):
                    nc.vector.tensor_copy(out=o_sb[:, pos * IN_F:(pos + 1) * IN_F], in_=acc[:])
                else:
                    nc.scalar.copy(out=o_sb[:, pos * IN_F:(pos + 1) * IN_F], in_=acc[:])
                if pos == STORES[k] - 1:
                    c0 = (j + 1 - STORES[k]) * IN_F
                    nc.sync.dma_start(out=o_flat[:, c0:c0 + STORES[k] * IN_F], in_=o_sb[:])

        build_weight()
        for n in range(N_EARLY):
            transposes(n)
        quantise(0)
        quantise_weight()
        quantise(1)
        for n in range(N_GROUPS):
            if n + 2 < N_GROUPS:
                quantise(n + 2)
            if n + N_EARLY < N_GROUPS:
                transposes(n + N_EARLY)
            multiply(n)
